import numpy as np
import ml_dtypes


def mxq(x, axis, fmt="e4m3"):
    dtype, down = {"e4m3": (ml_dtypes.float8_e4m3fn, 7), "e5m2": (ml_dtypes.float8_e5m2, 14)}[fmt]
    v = np.moveaxis(np.asarray(x, np.float32).astype(ml_dtypes.bfloat16).astype(np.float64), axis, -1)
    blocks = v.reshape(v.shape[:-1] + (-1, 32))
    amax = np.abs(blocks).max(-1, keepdims=True)
    byte = np.maximum(np.where(amax > 0, np.frexp(amax)[1] - 1 + 127, 0) - down, 1)
    scale = np.exp2(byte - 127.0)
    codes = (blocks / scale).astype(np.float32).astype(dtype).astype(np.float64)
    return np.moveaxis((codes * scale).reshape(v.shape), -1, axis)


WIDE = False


def mx_kscale(k):
    if not WIDE:
        return np.ones(k)
    levels = np.array([10, -10, 5, -5, 0])
    a = np.random.permutation(np.resize(levels, k // 512 * 4)).reshape(k // 512, 4)
    idx = np.arange(k)
    return np.exp2(a[idx // 512, idx % 128 // 32])


BF16 = ml_dtypes.bfloat16


def bf(x):
    return np.asarray(x, np.float32).astype(BF16)


def f64(x):
    return np.asarray(x).astype(np.float64)


G, S, M, H, E, C = 4, 1024, 512, 512, 16, 64


def setup_inputs():
    t = mx_kscale(H)
    u = mx_kscale(E * C).reshape(E, C)
    return {"h": bf(np.maximum(np.random.standard_normal((E, G, C, H)), 0.0) * 1.4 * t * u[:, None, :, None]),
            "wo": bf(np.random.standard_normal((E, H, M)) * 10.0 / np.sqrt(H * E * C) / t[None, :, None]),
            "combined_weights": bf(np.random.standard_normal((G, S, E, C)) * 0.1 / u)}


def reference(h, wo, combined_weights):
    eo = mxq(f64(h).reshape(E, G * C, H), 2, "e4m3") @ mxq(f64(wo), 1, "e4m3")
    expert_outputs = eo.reshape(E, G, C, M).transpose(1, 0, 2, 3)
    cw = mxq(f64(combined_weights).reshape(G, S, E * C), 2, "e4m3")
    return cw @ mxq(expert_outputs.reshape(G, E * C, M), 1, "e4m3")

@@ -1,0 +1,182 @@
+from contextlib import ExitStack
+
+from concourse import mybir
+from concourse.masks import make_identity
+
+BF16 = mybir.dt.bfloat16
+F32 = mybir.dt.float32
+I32 = mybir.dt.int32
+U32 = mybir.dt.uint32
+U8 = mybir.dt.uint8
+FP8X4 = mybir.dt.float8_e4m3fn_x4
+
+E, G, C, H, M, S = 16, 4, 64, 512, 512, 1024
+P = 128
+PACK = 4
+K_PASS = P * PACK
+K2 = E * C
+PASSES2 = K2 // K_PASS
+S_TILES = S // P
+M_CHUNKS = M // P
+TILES_PER_LOAD = 2
+
+FLOPS = 2 * E * G * C * H * M + 2 * G * S * K2 * M
+
+
+def tile_flaxpositionwisemoelayer_pb_t_kernel(tc, h, wo, combined_weights, out):
+    nc = tc.nc
+    with ExitStack() as ctx:
+        const = ctx.enter_context(tc.tile_pool(name="const", bufs=1))
+        keep = ctx.enter_context(tc.tile_pool(name="keep", bufs=1))
+        raw = ctx.enter_context(tc.tile_pool(name="raw", bufs=4))
+        grouped = ctx.enter_context(tc.tile_pool(name="grouped", bufs=2))
+        result = ctx.enter_context(tc.tile_pool(name="result", bufs=3))
+        flip = ctx.enter_context(tc.psum_pool(name="flip", bufs=4))
+        sums = ctx.enter_context(tc.psum_pool(name="sums", bufs=2))
+
+        ident_bf16 = const.tile([P, P], BF16)
+        make_identity(nc, ident_bf16[:])
+        ident_f32 = const.tile([P, P], F32)
+        make_identity(nc, ident_f32[:])
+
+        wo_codes = keep.tile([P, E, M], U32, align_bytes=64)
+        wo_scales = keep.tile([P, E, M], U8, align_bytes=64)
+        h_codes = keep.tile([P, E, G, P], U32, align_bytes=64)
+        h_scales = keep.tile([P, E, G, P], U8, align_bytes=64)
+        cw_codes = keep.tile([P, G, S_TILES, PASSES2 * P], U32, align_bytes=64)
+        cw_scales = keep.tile([P, G, S_TILES, PASSES2 * P], U8, align_bytes=64)
+        eo_codes = keep.tile([P, G, PASSES2, M], U32, align_bytes=64)
+        eo_scales = keep.tile([P, G, PASSES2, M], U8, align_bytes=64)
+
+        for parity in range(2):
+            empty = slice((1 - parity) * C, (2 - parity) * C)
+            nc.vector.memset(
+                h_codes[:].bitcast(I32).rearrange("p (a b) g c -> p a b g c", b=2)[:, :, parity, :, empty], 0
+            )
+            empty_bytes = slice((1 - parity) * C // 4, (2 - parity) * C // 4)
+            nc.vector.memset(
+                h_scales[:].bitcast(I32).rearrange("p (a b) g c -> p a b g c", b=2)[:, :, parity, :, empty_bytes], 0
+            )
+
+        def quantise_wo(e):
+            wo_raw = raw.tile([P, PACK, M], BF16)
+            nc.sync.dma_start(
+                out=wo_raw[:].rearrange("p (u i) m -> p u (i m)", i=2),
+                in_=wo[e].rearrange("(u p i) m -> p u (i m)", u=2, i=2),
+            )
+            wo_grouped = grouped.tile([P, M, PACK], BF16, align_bytes=64)
+            nc.vector.tensor_copy(
+                out=wo_grouped[:].rearrange("p (c i) t -> p c t i", i=4),
+                in_=wo_raw[:].rearrange("p t (c i) -> p c t i", i=4),
+            )
+            nc.vector.quantize_mx(
+                out=wo_codes[:, e, :].bitcast(FP8X4),
+                scales=wo_scales[:, e, :],
+                in_=wo_grouped[:].rearrange("p m t -> p (m t)"),
+            )
+
+        def quantise_h(e):
+            h_raw = raw.tile([P, 2 * H], BF16)
+            nc.sync.dma_start(out=h_raw[:], in_=h[e].rearrange("g (d n) k -> (g d) (n k)", n=2))
+            h_words = h_raw[:].bitcast(F32)
+            h_flip = flip.tile([P, 2, 2, P], F32, tag="flip")
+            for n in range(2):
+                for u in range(2):
+                    first = (2 * n + u) * P
+                    nc.tensor.transpose(h_flip[:, n, u, :], h_words[:, first : first + P], ident_f32[:])
+            h_grouped = grouped.tile([P, G * C * PACK], BF16, align_bytes=64)
+            nc.scalar.copy(
+                out=h_grouped[:].bitcast(F32).rearrange("p (r n u) -> p r n u", n=2, u=2),
+                in_=h_flip[:].rearrange("p n u r -> p r n u"),
+            )
+            half = slice((e % 2) * C, (e % 2 + 1) * C)
+            for g in range(G):
+                nc.vector.quantize_mx(
+                    out=h_codes[:, e, g, half].bitcast(FP8X4),
+                    scales=h_scales[:, e, g, half],
+                    in_=h_grouped[:, g * C * PACK : (g + 1) * C * PACK],
+                )
+
+        def quantise_cw(g, first_tile):
+            cw_raw = raw.tile([P, TILES_PER_LOAD, K2], BF16)
+            nc.sync.dma_start(
+                out=cw_raw[:],
+                in_=combined_weights[g].rearrange("(r n) e c -> r n (e c)", n=S_TILES)[
+                    :, first_tile : first_tile + TILES_PER_LOAD, :
+                ],
+            )
+            for j in range(TILES_PER_LOAD):
+                cw_flip = flip.tile([P, PASSES2 * PACK, P], BF16, tag="flip")
+                for w in range(PASSES2 * PACK):
+                    nc.tensor.transpose(cw_flip[:, w, :], cw_raw[:, j, w * P : (w + 1) * P], ident_bf16[:])
+                cw_grouped = grouped.tile([P, PASSES2, P, PACK], BF16, align_bytes=64)
+                nc.scalar.copy(out=cw_grouped[:], in_=cw_flip[:].rearrange("p (a t) r -> p a r t", t=PACK))
+                nc.vector.quantize_mx(
+                    out=cw_codes[:, g, first_tile + j, :].bitcast(FP8X4),
+                    scales=cw_scales[:, g, first_tile + j, :],
+                    in_=cw_grouped[:].rearrange("p a r t -> p (a r t)"),
+                )
+
+        def copy_out(turn, dst, src):
+            if turn % 2 == 0:
+                nc.scalar.copy(out=dst, in_=src)
+            else:
+                nc.vector.tensor_copy(out=dst, in_=src)
+
+        def expert_outputs(a, g):
+            eo_grouped = grouped.tile([P, M_CHUNKS, P, PACK], BF16, align_bytes=64)
+            for mc in range(M_CHUNKS):
+                cols = slice(mc * P, (mc + 1) * P)
+                eo_sum = sums.tile([P, PACK, P], F32)
+                for t in range(PACK):
+                    for parity in range(2):
+                        e = (K_PASS // C) * a + 2 * t + parity
+                        nc.tensor.matmul_mx(
+                            out=eo_sum[:, t, :],
+                            lhsT=h_codes[:, e, g, :].bitcast(FP8X4),
+                            lhsT_scale=h_scales[:, e, g, :],
+                            rhs=wo_codes[:, e, cols].bitcast(FP8X4),
+                            rhs_scale=wo_scales[:, e, cols],
+                            start=(parity == 0),
+                            stop=(parity == 1),
+                        )
+                copy_out(mc, eo_grouped[:, mc, :, :], eo_sum[:].rearrange("p t m -> p m t"))
+            nc.vector.quantize_mx(
+                out=eo_codes[:, g, a, :].bitcast(FP8X4),
+                scales=eo_scales[:, g, a, :],
+                in_=eo_grouped[:].rearrange("p q m t -> p (q m t)"),
+            )
+
+        def combine(g):
+            out_rows = out[g].rearrange("(r n) m -> r n m", n=S_TILES)
+            for first_tile in range(0, S_TILES, TILES_PER_LOAD):
+                out_sb = result.tile([P, TILES_PER_LOAD, M], F32)
+                for j in range(TILES_PER_LOAD):
+                    out_sum = sums.tile([P, M], F32)
+                    for a in range(PASSES2):
+                        cols = slice(a * P, (a + 1) * P)
+                        nc.tensor.matmul_mx(
+                            out=out_sum[:],
+                            lhsT=cw_codes[:, g, first_tile + j, cols].bitcast(FP8X4),
+                            lhsT_scale=cw_scales[:, g, first_tile + j, cols],
+                            rhs=eo_codes[:, g, a, :].bitcast(FP8X4),
+                            rhs_scale=eo_scales[:, g, a, :],
+                            start=(a == 0),
+                            stop=(a == PASSES2 - 1),
+                        )
+                    copy_out(j, out_sb[:, j, :], out_sum[:])
+                nc.sync.dma_start(out=out_rows[:, first_tile : first_tile + TILES_PER_LOAD, :], in_=out_sb[:])
+
+        loads_per_group = S_TILES // TILES_PER_LOAD
+        for e in range(E):
+            quantise_wo(e)
+            quantise_h(e)
+            quantise_cw(e // loads_per_group, (e % loads_per_group) * TILES_PER_LOAD)
+            if e == E // 2 - 1:
+                for g in range(G):
+                    expert_outputs(0, g)
+        expert_outputs(1, 0)
+        for g in range(G):
+            if g + 1 < G:
+                expert_outputs(1, g + 1)
+            combine(g)

@@ -31,8 +31,8 @@ def tile_flaxpositionwisemoelayer_pb_t_kernel(tc, h, wo, combined_weights, out):
         raw = ctx.enter_context(tc.tile_pool(name="raw", bufs=4))
         grouped = ctx.enter_context(tc.tile_pool(name="grouped", bufs=2))
         result = ctx.enter_context(tc.tile_pool(name="result", bufs=3))
-        flip = ctx.enter_context(tc.psum_pool(name="flip", bufs=4))
-        sums = ctx.enter_context(tc.psum_pool(name="sums", bufs=2))
+        banks = ctx.enter_context(tc.psum_pool(name="banks", bufs=8))
+        ctx.enter_context(tc.manual_schedule())
 
         ident_bf16 = const.tile([P, P], BF16)
         make_identity(nc, ident_bf16[:])
@@ -58,28 +58,86 @@ def tile_flaxpositionwisemoelayer_pb_t_kernel(tc, h, wo, combined_weights, out):
                 h_scales[:].bitcast(I32).rearrange("p (a b) g c -> p a b g c", b=2)[:, :, parity, :, empty_bytes], 0
             )
 
-        def quantise_wo(e):
+        def copy_out(turn, dst, src):
+            if turn % 2 == 0:
+                nc.scalar.copy(out=dst, in_=src)
+            else:
+                nc.vector.tensor_copy(out=dst, in_=src)
+
+        def expert_outputs(a, g, eo_grouped, chunks):
+            for mc in chunks:
+                cols = slice(mc * P, (mc + 1) * P)
+                eo_sum = banks.tile([P, PACK, P], F32, tag="bank")
+                for t in range(PACK):
+                    for parity in range(2):
+                        e = (K_PASS // C) * a + 2 * t + parity
+                        nc.tensor.matmul_mx(
+                            out=eo_sum[:, t, :],
+                            lhsT=h_codes[:, e, g, :].bitcast(FP8X4),
+                            lhsT_scale=h_scales[:, e, g, :],
+                            rhs=wo_codes[:, e, cols].bitcast(FP8X4),
+                            rhs_scale=wo_scales[:, e, cols],
+                            start=(parity == 0),
+                            stop=(parity == 1),
+                        )
+                copy_out(mc, eo_grouped[:, mc, :, :], eo_sum[:].rearrange("p t m -> p m t"))
+
+        def quantise_expert_outputs(a, g, eo_grouped):
+            nc.vector.quantize_mx(
+                out=eo_codes[:, g, a, :].bitcast(FP8X4),
+                scales=eo_scales[:, g, a, :],
+                in_=eo_grouped[:].rearrange("p q m t -> p (q m t)"),
+            )
+
+        def combine(g):
+            out_rows = out[g].rearrange("(r n) m -> r n m", n=S_TILES)
+            for first_tile in range(0, S_TILES, TILES_PER_LOAD):
+                out_sb = result.tile([P, TILES_PER_LOAD, M], F32)
+                for j in range(TILES_PER_LOAD):
+                    out_sum = banks.tile([P, M], F32, tag="bank")
+                    for a in range(PASSES2):
+                        cols = slice(a * P, (a + 1) * P)
+                        nc.tensor.matmul_mx(
+                            out=out_sum[:],
+                            lhsT=cw_codes[:, g, first_tile + j, cols].bitcast(FP8X4),
+                            lhsT_scale=cw_scales[:, g, first_tile + j, cols],
+                            rhs=eo_codes[:, g, a, :].bitcast(FP8X4),
+                            rhs_scale=eo_scales[:, g, a, :],
+                            start=(a == 0),
+                            stop=(a == PASSES2 - 1),
+                        )
+                    copy_out(j, out_sb[:, j, :], out_sum[:])
+                nc.sync.dma_start(out=out_rows[:, first_tile : first_tile + TILES_PER_LOAD, :], in_=out_sb[:])
+
+        loads_per_group = S_TILES // TILES_PER_LOAD
+        eo_first = None
+        for e in range(E):
+            g_cw = e // loads_per_group
+            first_tile = (e % loads_per_group) * TILES_PER_LOAD
+
             wo_raw = raw.tile([P, PACK, M], BF16)
             nc.sync.dma_start(
                 out=wo_raw[:].rearrange("p (u i) m -> p u (i m)", i=2),
                 in_=wo[e].rearrange("(u p i) m -> p u (i m)", u=2, i=2),
             )
+            h_raw = raw.tile([P, 2 * H], BF16)
+            nc.sync.dma_start(out=h_raw[:], in_=h[e].rearrange("g (d n) k -> (g d) (n k)", n=2))
+            cw_raw = raw.tile([P, TILES_PER_LOAD, K2], BF16)
+            nc.sync.dma_start(
+                out=cw_raw[:],
+                in_=combined_weights[g_cw].rearrange("(r n) e c -> r n (e c)", n=S_TILES)[
+                    :, first_tile : first_tile + TILES_PER_LOAD, :
+                ],
+            )
+
             wo_grouped = grouped.tile([P, M, PACK], BF16, align_bytes=64)
             nc.vector.tensor_copy(
                 out=wo_grouped[:].rearrange("p (c i) t -> p c t i", i=4),
                 in_=wo_raw[:].rearrange("p t (c i) -> p c t i", i=4),
             )
-            nc.vector.quantize_mx(
-                out=wo_codes[:, e, :].bitcast(FP8X4),
-                scales=wo_scales[:, e, :],
-                in_=wo_grouped[:].rearrange("p m t -> p (m t)"),
-            )
 
-        def quantise_h(e):
-            h_raw = raw.tile([P, 2 * H], BF16)
-            nc.sync.dma_start(out=h_raw[:], in_=h[e].rearrange("g (d n) k -> (g d) (n k)", n=2))
             h_words = h_raw[:].bitcast(F32)
-            h_flip = flip.tile([P, 2, 2, P], F32, tag="flip")
+            h_flip = banks.tile([P, 2, 2, P], F32, tag="bank")
             for n in range(2):
                 for u in range(2):
                     first = (2 * n + u) * P
@@ -97,86 +155,39 @@ def tile_flaxpositionwisemoelayer_pb_t_kernel(tc, h, wo, combined_weights, out):
                     in_=h_grouped[:, g * C * PACK : (g + 1) * C * PACK],
                 )
 
-        def quantise_cw(g, first_tile):
-            cw_raw = raw.tile([P, TILES_PER_LOAD, K2], BF16)
-            nc.sync.dma_start(
-                out=cw_raw[:],
-                in_=combined_weights[g].rearrange("(r n) e c -> r n (e c)", n=S_TILES)[
-                    :, first_tile : first_tile + TILES_PER_LOAD, :
-                ],
-            )
             for j in range(TILES_PER_LOAD):
-                cw_flip = flip.tile([P, PASSES2 * PACK, P], BF16, tag="flip")
-                for w in range(PASSES2 * PACK):
-                    nc.tensor.transpose(cw_flip[:, w, :], cw_raw[:, j, w * P : (w + 1) * P], ident_bf16[:])
                 cw_grouped = grouped.tile([P, PASSES2, P, PACK], BF16, align_bytes=64)
-                nc.scalar.copy(out=cw_grouped[:], in_=cw_flip[:].rearrange("p (a t) r -> p a r t", t=PACK))
+                for a in range(PASSES2):
+                    cw_flip = banks.tile([P, PACK, P], BF16, tag="bank")
+                    for t in range(PACK):
+                        w = PACK * a + t
+                        nc.tensor.transpose(cw_flip[:, t, :], cw_raw[:, j, w * P : (w + 1) * P], ident_bf16[:])
+                    nc.scalar.copy(out=cw_grouped[:, a, :, :], in_=cw_flip[:].rearrange("p t r -> p r t"))
                 nc.vector.quantize_mx(
-                    out=cw_codes[:, g, first_tile + j, :].bitcast(FP8X4),
-                    scales=cw_scales[:, g, first_tile + j, :],
+                    out=cw_codes[:, g_cw, first_tile + j, :].bitcast(FP8X4),
+                    scales=cw_scales[:, g_cw, first_tile + j, :],
                     in_=cw_grouped[:].rearrange("p a r t -> p (a r t)"),
                 )
 
-        def copy_out(turn, dst, src):
-            if turn % 2 == 0:
-                nc.scalar.copy(out=dst, in_=src)
-            else:
-                nc.vector.tensor_copy(out=dst, in_=src)
-
-        def expert_outputs(a, g):
-            eo_grouped = grouped.tile([P, M_CHUNKS, P, PACK], BF16, align_bytes=64)
-            for mc in range(M_CHUNKS):
-                cols = slice(mc * P, (mc + 1) * P)
-                eo_sum = sums.tile([P, PACK, P], F32)
-                for t in range(PACK):
-                    for parity in range(2):
-                        e = (K_PASS // C) * a + 2 * t + parity
-                        nc.tensor.matmul_mx(
-                            out=eo_sum[:, t, :],
-                            lhsT=h_codes[:, e, g, :].bitcast(FP8X4),
-                            lhsT_scale=h_scales[:, e, g, :],
-                            rhs=wo_codes[:, e, cols].bitcast(FP8X4),
-                            rhs_scale=wo_scales[:, e, cols],
-                            start=(parity == 0),
-                            stop=(parity == 1),
-                        )
-                copy_out(mc, eo_grouped[:, mc, :, :], eo_sum[:].rearrange("p t m -> p m t"))
             nc.vector.quantize_mx(
-                out=eo_codes[:, g, a, :].bitcast(FP8X4),
-                scales=eo_scales[:, g, a, :],
-                in_=eo_grouped[:].rearrange("p q m t -> p (q m t)"),
+                out=wo_codes[:, e, :].bitcast(FP8X4),
+                scales=wo_scales[:, e, :],
+                in_=wo_grouped[:].rearrange("p m t -> p (m t)"),
             )
 
-        def combine(g):
-            out_rows = out[g].rearrange("(r n) m -> r n m", n=S_TILES)
-            for first_tile in range(0, S_TILES, TILES_PER_LOAD):
-                out_sb = result.tile([P, TILES_PER_LOAD, M], F32)
-                for j in range(TILES_PER_LOAD):
-                    out_sum = sums.tile([P, M], F32)
-                    for a in range(PASSES2):
-                        cols = slice(a * P, (a + 1) * P)
-                        nc.tensor.matmul_mx(
-                            out=out_sum[:],
-                            lhsT=cw_codes[:, g, first_tile + j, cols].bitcast(FP8X4),
-                            lhsT_scale=cw_scales[:, g, first_tile + j, cols],
-                            rhs=eo_codes[:, g, a, :].bitcast(FP8X4),
-                            rhs_scale=eo_scales[:, g, a, :],
-                            start=(a == 0),
-                            stop=(a == PASSES2 - 1),
-                        )
-                    copy_out(j, out_sb[:, j, :], out_sum[:])
-                nc.sync.dma_start(out=out_rows[:, first_tile : first_tile + TILES_PER_LOAD, :], in_=out_sb[:])
+            if e >= E // 2:
+                g = (e - E // 2) // 2
+                if e % 2 == 0:
+                    eo_first = grouped.tile([P, M_CHUNKS, P, PACK], BF16, align_bytes=64, name="eo_grouped")
+                    expert_outputs(0, g, eo_first, range(0, M_CHUNKS // 2))
+                else:
+                    expert_outputs(0, g, eo_first, range(M_CHUNKS // 2, M_CHUNKS))
+                    quantise_expert_outputs(0, g, eo_first)
 
-        loads_per_group = S_TILES // TILES_PER_LOAD
-        for e in range(E):
-            quantise_wo(e)
-            quantise_h(e)
-            quantise_cw(e // loads_per_group, (e % loads_per_group) * TILES_PER_LOAD)
-            if e == E // 2 - 1:
-                for g in range(G):
-                    expert_outputs(0, g)
-        expert_outputs(1, 0)
-        for g in range(G):
-            if g + 1 < G:
-                expert_outputs(1, g + 1)
-            combine(g)
+        for g in range(G + 1):
+            if g < G:
+                eo_second = grouped.tile([P, M_CHUNKS, P, PACK], BF16, align_bytes=64, name="eo_grouped")
+                expert_outputs(1, g, eo_second, range(M_CHUNKS))
+                quantise_expert_outputs(1, g, eo_second)
+            if g > 0:
+                combine(g - 1)

@@ -30,6 +30,7 @@ def tile_flaxpositionwisemoelayer_pb_t_kernel(tc, h, wo, combined_weights, out):
         keep = ctx.enter_context(tc.tile_pool(name="keep", bufs=1))
         raw = ctx.enter_context(tc.tile_pool(name="raw", bufs=4))
         grouped = ctx.enter_context(tc.tile_pool(name="grouped", bufs=2))
+        cw_pool = ctx.enter_context(tc.tile_pool(name="cw_pool", bufs=4))
         result = ctx.enter_context(tc.tile_pool(name="result", bufs=3))
         banks = ctx.enter_context(tc.psum_pool(name="banks", bufs=8))
         ctx.enter_context(tc.manual_schedule())
@@ -110,7 +111,6 @@ def tile_flaxpositionwisemoelayer_pb_t_kernel(tc, h, wo, combined_weights, out):
                 nc.sync.dma_start(out=out_rows[:, first_tile : first_tile + TILES_PER_LOAD, :], in_=out_sb[:])
 
         loads_per_group = S_TILES // TILES_PER_LOAD
-        eo_first = None
         for e in range(E):
             g_cw = e // loads_per_group
             first_tile = (e % loads_per_group) * TILES_PER_LOAD
@@ -155,8 +155,14 @@ def tile_flaxpositionwisemoelayer_pb_t_kernel(tc, h, wo, combined_weights, out):
                     in_=h_grouped[:, g * C * PACK : (g + 1) * C * PACK],
                 )
 
+            nc.vector.quantize_mx(
+                out=wo_codes[:, e, :].bitcast(FP8X4),
+                scales=wo_scales[:, e, :],
+                in_=wo_grouped[:].rearrange("p m t -> p (m t)"),
+            )
+
             for j in range(TILES_PER_LOAD):
-                cw_grouped = grouped.tile([P, PASSES2, P, PACK], BF16, align_bytes=64)
+                cw_grouped = cw_pool.tile([P, PASSES2, P, PACK], BF16, align_bytes=64)
                 for a in range(PASSES2):
                     cw_flip = banks.tile([P, PACK, P], BF16, tag="bank")
                     for t in range(PACK):
@@ -169,20 +175,11 @@ def tile_flaxpositionwisemoelayer_pb_t_kernel(tc, h, wo, combined_weights, out):
                     in_=cw_grouped[:].rearrange("p a r t -> p (a r t)"),
                 )
 
-            nc.vector.quantize_mx(
-                out=wo_codes[:, e, :].bitcast(FP8X4),
-                scales=wo_scales[:, e, :],
-                in_=wo_grouped[:].rearrange("p m t -> p (m t)"),
-            )
-
-            if e >= E // 2:
+            if e >= E // 2 and e % 2 == 0:
                 g = (e - E // 2) // 2
-                if e % 2 == 0:
-                    eo_first = grouped.tile([P, M_CHUNKS, P, PACK], BF16, align_bytes=64, name="eo_grouped")
-                    expert_outputs(0, g, eo_first, range(0, M_CHUNKS // 2))
-                else:
-                    expert_outputs(0, g, eo_first, range(M_CHUNKS // 2, M_CHUNKS))
-                    quantise_expert_outputs(0, g, eo_first)
+                eo_first = grouped.tile([P, M_CHUNKS, P, PACK], BF16, align_bytes=64, name="eo_grouped")
+                expert_outputs(0, g, eo_first, range(M_CHUNKS))
+                quantise_expert_outputs(0, g, eo_first)
 
         for g in range(G + 1):
             if g < G:

from contextlib import ExitStack

from concourse import mybir
from concourse.masks import make_identity

BF16 = mybir.dt.bfloat16
F32 = mybir.dt.float32
I32 = mybir.dt.int32
U32 = mybir.dt.uint32
U8 = mybir.dt.uint8
FP8X4 = mybir.dt.float8_e4m3fn_x4

E, G, C, H, M, S = 16, 4, 64, 512, 512, 1024
P = 128
PACK = 4
K_PASS = P * PACK
K2 = E * C
PASSES2 = K2 // K_PASS
S_TILES = S // P
M_CHUNKS = M // P
TILES_PER_LOAD = 2

FLOPS = 2 * E * G * C * H * M + 2 * G * S * K2 * M


def tile_flaxpositionwisemoelayer_pb_t_kernel(tc, h, wo, combined_weights, out):
    nc = tc.nc
    with ExitStack() as ctx:
        const = ctx.enter_context(tc.tile_pool(name="const", bufs=1))
        keep = ctx.enter_context(tc.tile_pool(name="keep", bufs=1))
        raw = ctx.enter_context(tc.tile_pool(name="raw", bufs=4))
        grouped = ctx.enter_context(tc.tile_pool(name="grouped", bufs=2))
        cw_pool = ctx.enter_context(tc.tile_pool(name="cw_pool", bufs=4))
        result = ctx.enter_context(tc.tile_pool(name="result", bufs=3))
        banks = ctx.enter_context(tc.psum_pool(name="banks", bufs=8))
        ctx.enter_context(tc.manual_schedule())

        ident_bf16 = const.tile([P, P], BF16)
        make_identity(nc, ident_bf16[:])
        ident_f32 = const.tile([P, P], F32)
        make_identity(nc, ident_f32[:])

        wo_codes = keep.tile([P, E, M], U32, align_bytes=64)
        wo_scales = keep.tile([P, E, M], U8, align_bytes=64)
        h_codes = keep.tile([P, E, G, P], U32, align_bytes=64)
        h_scales = keep.tile([P, E, G, P], U8, align_bytes=64)
        cw_codes = keep.tile([P, G, S_TILES, PASSES2 * P], U32, align_bytes=64)
        cw_scales = keep.tile([P, G, S_TILES, PASSES2 * P], U8, align_bytes=64)
        eo_codes = keep.tile([P, G, PASSES2, M], U32, align_bytes=64)
        eo_scales = keep.tile([P, G, PASSES2, M], U8, align_bytes=64)

        for parity in range(2):
            empty = slice((1 - parity) * C, (2 - parity) * C)
            nc.vector.memset(
                h_codes[:].bitcast(I32).rearrange("p (a b) g c -> p a b g c", b=2)[:, :, parity, :, empty], 0
            )
            empty_bytes = slice((1 - parity) * C // 4, (2 - parity) * C // 4)
            nc.vector.memset(
                h_scales[:].bitcast(I32).rearrange("p (a b) g c -> p a b g c", b=2)[:, :, parity, :, empty_bytes], 0
            )

        def copy_out(turn, dst, src):
            if turn % 2 == 0:
                nc.scalar.copy(out=dst, in_=src)
            else:
                nc.vector.tensor_copy(out=dst, in_=src)

        def expert_outputs(a, g, eo_grouped, chunks):
            for mc in chunks:
                cols = slice(mc * P, (mc + 1) * P)
                eo_sum = banks.tile([P, PACK, P], F32, tag="bank")
                for t in range(PACK):
                    for parity in range(2):
                        e = (K_PASS // C) * a + 2 * t + parity
                        nc.tensor.matmul_mx(
                            out=eo_sum[:, t, :],
                            lhsT=h_codes[:, e, g, :].bitcast(FP8X4),
                            lhsT_scale=h_scales[:, e, g, :],
                            rhs=wo_codes[:, e, cols].bitcast(FP8X4),
                            rhs_scale=wo_scales[:, e, cols],
                            start=(parity == 0),
                            stop=(parity == 1),
                        )
                copy_out(mc, eo_grouped[:, mc, :, :], eo_sum[:].rearrange("p t m -> p m t"))

        def quantise_expert_outputs(a, g, eo_grouped):
            nc.vector.quantize_mx(
                out=eo_codes[:, g, a, :].bitcast(FP8X4),
                scales=eo_scales[:, g, a, :],
                in_=eo_grouped[:].rearrange("p q m t -> p (q m t)"),
            )

        def combine(g):
            out_rows = out[g].rearrange("(r n) m -> r n m", n=S_TILES)
            for first_tile in range(0, S_TILES, TILES_PER_LOAD):
                out_sb = result.tile([P, TILES_PER_LOAD, M], F32)
                for j in range(TILES_PER_LOAD):
                    out_sum = banks.tile([P, M], F32, tag="bank")
                    for a in range(PASSES2):
                        cols = slice(a * P, (a + 1) * P)
                        nc.tensor.matmul_mx(
                            out=out_sum[:],
                            lhsT=cw_codes[:, g, first_tile + j, cols].bitcast(FP8X4),
                            lhsT_scale=cw_scales[:, g, first_tile + j, cols],
                            rhs=eo_codes[:, g, a, :].bitcast(FP8X4),
                            rhs_scale=eo_scales[:, g, a, :],
                            start=(a == 0),
                            stop=(a == PASSES2 - 1),
                        )
                    copy_out(j, out_sb[:, j, :], out_sum[:])
                nc.sync.dma_start(out=out_rows[:, first_tile : first_tile + TILES_PER_LOAD, :], in_=out_sb[:])

        loads_per_group = S_TILES // TILES_PER_LOAD
        for e in range(E):
            g_cw = e // loads_per_group
            first_tile = (e % loads_per_group) * TILES_PER_LOAD

            wo_raw = raw.tile([P, PACK, M], BF16)
            nc.sync.dma_start(
                out=wo_raw[:].rearrange("p (u i) m -> p u (i m)", i=2),
                in_=wo[e].rearrange("(u p i) m -> p u (i m)", u=2, i=2),
            )
            h_raw = raw.tile([P, 2 * H], BF16)
            nc.sync.dma_start(out=h_raw[:], in_=h[e].rearrange("g (d n) k -> (g d) (n k)", n=2))
            cw_raw = raw.tile([P, TILES_PER_LOAD, K2], BF16)
            nc.sync.dma_start(
                out=cw_raw[:],
                in_=combined_weights[g_cw].rearrange("(r n) e c -> r n (e c)", n=S_TILES)[
                    :, first_tile : first_tile + TILES_PER_LOAD, :
                ],
            )

            wo_grouped = grouped.tile([P, M, PACK], BF16, align_bytes=64)
            nc.vector.tensor_copy(
                out=wo_grouped[:].rearrange("p (c i) t -> p c t i", i=4),
                in_=wo_raw[:].rearrange("p t (c i) -> p c t i", i=4),
            )

            h_words = h_raw[:].bitcast(F32)
            h_flip = banks.tile([P, 2, 2, P], F32, tag="bank")
            for n in range(2):
                for u in range(2):
                    first = (2 * n + u) * P
                    nc.tensor.transpose(h_flip[:, n, u, :], h_words[:, first : first + P], ident_f32[:])
            h_grouped = grouped.tile([P, G * C * PACK], BF16, align_bytes=64)
            nc.scalar.copy(
                out=h_grouped[:].bitcast(F32).rearrange("p (r n u) -> p r n u", n=2, u=2),
                in_=h_flip[:].rearrange("p n u r -> p r n u"),
            )
            half = slice((e % 2) * C, (e % 2 + 1) * C)
            for g in range(G):
                nc.vector.quantize_mx(
                    out=h_codes[:, e, g, half].bitcast(FP8X4),
                    scales=h_scales[:, e, g, half],
                    in_=h_grouped[:, g * C * PACK : (g + 1) * C * PACK],
                )

            nc.vector.quantize_mx(
                out=wo_codes[:, e, :].bitcast(FP8X4),
                scales=wo_scales[:, e, :],
                in_=wo_grouped[:].rearrange("p m t -> p (m t)"),
            )

            for j in range(TILES_PER_LOAD):
                cw_grouped = cw_pool.tile([P, PASSES2, P, PACK], BF16, align_bytes=64)
                for a in range(PASSES2):
                    cw_flip = banks.tile([P, PACK, P], BF16, tag="bank")
                    for t in range(PACK):
                        w = PACK * a + t
                        nc.tensor.transpose(cw_flip[:, t, :], cw_raw[:, j, w * P : (w + 1) * P], ident_bf16[:])
                    nc.scalar.copy(out=cw_grouped[:, a, :, :], in_=cw_flip[:].rearrange("p t r -> p r t"))
                nc.vector.quantize_mx(
                    out=cw_codes[:, g_cw, first_tile + j, :].bitcast(FP8X4),
                    scales=cw_scales[:, g_cw, first_tile + j, :],
                    in_=cw_grouped[:].rearrange("p a r t -> p (a r t)"),
                )

            if e >= E // 2 and e % 2 == 0:
                g = (e - E // 2) // 2
                eo_first = grouped.tile([P, M_CHUNKS, P, PACK], BF16, align_bytes=64, name="eo_grouped")
                expert_outputs(0, g, eo_first, range(M_CHUNKS))
                quantise_expert_outputs(0, g, eo_first)

        for g in range(G + 1):
            if g < G:
                eo_second = grouped.tile([P, M_CHUNKS, P, PACK], BF16, align_bytes=64, name="eo_grouped")
                expert_outputs(1, g, eo_second, range(M_CHUNKS))
                quantise_expert_outputs(1, g, eo_second)
            if g > 0:
                combine(g - 1)
